import numpy as np
import ml_dtypes

BF16 = ml_dtypes.bfloat16


def bf(x):
    return np.asarray(x, np.float32).astype(BF16)


def f32(x):
    return np.asarray(x, np.float32)


def f64(x):
    return np.asarray(x).astype(np.float64)


def striped(idx):
    return np.tile(idx.reshape(-1, 16).T, (8, 1))


D, V, T, HD, N, RUN, K = 512, 4096, 512, 128, 4096, 2048, 2
EPS = 1.1920928955078125e-07


def setup_inputs():
    emb = f32(np.random.standard_normal((D, V)))
    pos = f32(0.5 * np.random.standard_normal((D, T)))
    gain = f32(1.0 + 0.1 * np.random.standard_normal((D, 1)))
    wq = bf(np.random.standard_normal((D, D)) / np.sqrt(D))
    bq = f32(0.1 * np.random.standard_normal((D, 1)))
    wk = bf(np.random.standard_normal((D, HD)) / np.sqrt(D))
    bk = f32(0.1 * np.random.standard_normal((HD, 1)))
    wv = bf(np.random.standard_normal((D, D)) / np.sqrt(D))
    bv = f32(0.1 * np.random.standard_normal((D, 1)))
    idx = np.concatenate([np.random.permutation(V)[:RUN] for _ in range(K)])
    return {"emb": emb, "pos": pos, "gain": gain, "wq": wq, "bq": bq, "wk": wk, "bk": bk, "wv": wv, "bv": bv, "offs": striped(idx)}


def reference(emb, pos, gain, wq, bq, wk, bk, wv, bv, offs):
    idx = offs[:16].T.reshape(-1)
    h = f64(emb)[:, idx] + np.tile(f64(pos), (1, N // T))
    r = 1.0 / np.sqrt(np.mean(h * h, axis=0, keepdims=True) + EPS)
    x = h * r * f64(gain)
    qry = f64(wq).T @ x + f64(bq)
    key = f64(wk).T @ x + f64(bk)
    val = f64(wv).T @ x + f64(bv)
    return np.concatenate([h, qry, key, val], axis=0)

@@ -1,0 +1,126 @@
+import concourse.mybir as mybir
+from concourse.masks import make_identity
+
+F32, BF16, U16 = mybir.dt.float32, mybir.dt.bfloat16, mybir.dt.uint16
+ADD, MULT = mybir.AluOpType.add, mybir.AluOpType.mult
+ACT = mybir.ActivationFunctionType
+
+P = 128
+D, V, T, HD, N = 512, 4096, 512, 128, 4096
+EPS = 1.1920928955078125e-07
+KB = D // P
+MB = (D + HD + D) // P
+SEQS = N // T
+
+FLOPS = 2 * D * (D + HD + D) * N
+
+
+def tile_repro_b_kernel(tc, emb, pos, gain, wq, bq, wk, bk, wv, bv, offs, out):
+    nc = tc.nc
+    with (
+        tc.tile_pool(name="held", bufs=1) as held,
+        tc.tile_pool(name="squares", bufs=8) as squares,
+        tc.tile_pool(name="sums", bufs=4) as sums,
+        tc.tile_pool(name="norm", bufs=3) as norm,
+        tc.tile_pool(name="staged", bufs=8) as staged,
+    ):
+        offsets = held.tile([P, N // 16], U16, name="offsets")
+        nc.sync.dma_start(offsets[:], offs)
+
+        vec_rows = held.tile([P, P], F32, name="vec_rows")
+        nc.vector.memset(vec_rows[:], 0.0)
+        first_row = 0
+        for vec in (gain, bq, bk, bv):
+            rows = vec.rearrange("(m p) o -> m (p o)", p=P)
+            nc.sync.dma_start(vec_rows[first_row : first_row + rows.shape[0], :], rows)
+            first_row += rows.shape[0]
+
+        pos_sb = held.tile([P, KB, T], F32, name="pos_sb")
+        nc.sync.dma_start(pos_sb[:], pos.rearrange("(k p) t -> p k t", p=P))
+
+        tables = []
+        for k in range(KB):
+            table = held.tile([P, V], F32, name=f"table{k}")
+            nc.sync.dma_start(table[:], emb[k * P : (k + 1) * P, :])
+            tables.append(table)
+
+        weights = held.tile([P, KB, MB * P], BF16, name="weights")
+        first_col = 0
+        for w in (wq, wk, wv):
+            cols = w.shape[1]
+            nc.sync.dma_start(
+                weights[:, :, first_col : first_col + cols], w.rearrange("(k p) m -> p k m", p=P)
+            )
+            first_col += cols
+
+        mean_weights = held.tile([P, P], F32, name="mean_weights")
+        nc.vector.memset(mean_weights[:], 1.0 / D)
+        eps_col = held.tile([P, 1], F32, name="eps_col")
+        nc.vector.memset(eps_col[:], EPS)
+
+        identity = held.tile([P, P], F32, name="identity")
+        make_identity(nc, identity[:])
+        vec_cols = held.tile([P, KB + MB], F32, name="vec_cols")
+        with tc.psum_pool(name="setup_psum", bufs=1) as setup_psum:
+            flipped = setup_psum.tile([P, P], F32, name="flipped")
+            nc.tensor.transpose(flipped[:], vec_rows[:], identity[:])
+            nc.vector.tensor_copy(vec_cols[:], flipped[:, 0 : KB + MB])
+        gain_cols = [vec_cols[:, k : k + 1] for k in range(KB)]
+        bias_cols = [vec_cols[:, KB + m : KB + m + 1] for m in range(MB)]
+
+        hidden = [held.tile([P, N], F32, name=f"hidden{k}") for k in range(KB)]
+
+        with (
+            tc.psum_pool(name="mean_psum", bufs=2) as mean_psum,
+            tc.psum_pool(name="proj_psum", bufs=6) as proj_psum,
+        ):
+
+            def normalize(s):
+                span = slice(s * T, (s + 1) * T)
+                piece = offsets[:, s * (T // 16) : (s + 1) * (T // 16)]
+                total = sums.tile([P, T], F32, name="total")
+                for k in range(KB):
+                    h = hidden[k][:, span]
+                    nc.vector.tensor_tensor(h, tables[k][:].indirect(piece), pos_sb[:, k, :], ADD)
+                    nc.sync.dma_start(out[k * P : (k + 1) * P, span], h)
+                    if k == 0:
+                        nc.scalar.activation(total[:], h, ACT.Square)
+                    else:
+                        square = squares.tile([P, T], F32, name="square")
+                        nc.scalar.activation(square[:], h, ACT.Square)
+                        nc.vector.tensor_tensor(total[:], total[:], square[:], ADD)
+                mean = mean_psum.tile([P, T], F32, name="mean")
+                nc.tensor.matmul(mean[:], mean_weights[:], total[:], start=True, stop=True)
+                r = norm.tile([P, T], F32, name="r")
+                nc.scalar.activation(r[:], mean[:], ACT.Abs_reciprocal_sqrt, bias=eps_col[:])
+                xs = []
+                for k in range(KB):
+                    x = norm.tile([P, T], BF16, name=f"x{k}")
+                    nc.vector.scalar_tensor_tensor(
+                        x[:], hidden[k][:, span], gain_cols[k], r[:], MULT, MULT
+                    )
+                    xs.append(x)
+                return xs
+
+            def project(s, xs):
+                span = slice(s * T, (s + 1) * T)
+                for m in range(MB):
+                    acc = proj_psum.tile([P, T], F32, name="acc")
+                    for k in range(KB):
+                        nc.tensor.matmul(
+                            acc[:],
+                            weights[:, k, m * P : (m + 1) * P],
+                            xs[k][:],
+                            start=(k == 0),
+                            stop=(k == KB - 1),
+                        )
+                    y = staged.tile([P, T], F32, name="y")
+                    nc.scalar.activation(y[:], acc[:], ACT.Identity, bias=bias_cols[m])
+                    nc.sync.dma_start(out[D + m * P : D + (m + 1) * P, span], y[:])
+
+            xs_next = normalize(0)
+            for s in range(SEQS):
+                xs_now = xs_next
+                if s + 1 < SEQS:
+                    xs_next = normalize(s + 1)
+                project(s, xs_now)

@@ -19,6 +19,7 @@ def tile_repro_b_kernel(tc, emb, pos, gain, wq, bq, wk, bk, wv, bv, offs, out):
     nc = tc.nc
     with (
         tc.tile_pool(name="held", bufs=1) as held,
+        tc.tile_pool(name="hidden", bufs=3) as hidden,
         tc.tile_pool(name="squares", bufs=8) as squares,
         tc.tile_pool(name="sums", bufs=4) as sums,
         tc.tile_pool(name="norm", bufs=3) as norm,
@@ -32,7 +33,7 @@ def tile_repro_b_kernel(tc, emb, pos, gain, wq, bq, wk, bk, wv, bv, offs, out):
         first_row = 0
         for vec in (gain, bq, bk, bv):
             rows = vec.rearrange("(m p) o -> m (p o)", p=P)
-            nc.sync.dma_start(vec_rows[first_row : first_row + rows.shape[0], :], rows)
+            nc.scalar.dma_start(vec_rows[first_row : first_row + rows.shape[0], :], rows)
             first_row += rows.shape[0]
 
         pos_sb = held.tile([P, KB, T], F32, name="pos_sb")
@@ -68,8 +69,6 @@ def tile_repro_b_kernel(tc, emb, pos, gain, wq, bq, wk, bk, wv, bv, offs, out):
         gain_cols = [vec_cols[:, k : k + 1] for k in range(KB)]
         bias_cols = [vec_cols[:, KB + m : KB + m + 1] for m in range(MB)]
 
-        hidden = [held.tile([P, N], F32, name=f"hidden{k}") for k in range(KB)]
-
         with (
             tc.psum_pool(name="mean_psum", bufs=2) as mean_psum,
             tc.psum_pool(name="proj_psum", bufs=6) as proj_psum,
@@ -79,16 +78,18 @@ def tile_repro_b_kernel(tc, emb, pos, gain, wq, bq, wk, bk, wv, bv, offs, out):
                 span = slice(s * T, (s + 1) * T)
                 piece = offsets[:, s * (T // 16) : (s + 1) * (T // 16)]
                 total = sums.tile([P, T], F32, name="total")
+                hs = []
                 for k in range(KB):
-                    h = hidden[k][:, span]
-                    nc.vector.tensor_tensor(h, tables[k][:].indirect(piece), pos_sb[:, k, :], ADD)
-                    nc.sync.dma_start(out[k * P : (k + 1) * P, span], h)
+                    h = hidden.tile([P, T], F32, name=f"h{k}")
+                    nc.vector.tensor_tensor(h[:], tables[k][:].indirect(piece), pos_sb[:, k, :], ADD)
+                    nc.sync.dma_start(out[k * P : (k + 1) * P, span], h[:])
                     if k == 0:
-                        nc.scalar.activation(total[:], h, ACT.Square)
+                        nc.scalar.activation(total[:], h[:], ACT.Square)
                     else:
                         square = squares.tile([P, T], F32, name="square")
-                        nc.scalar.activation(square[:], h, ACT.Square)
+                        nc.scalar.activation(square[:], h[:], ACT.Square)
                         nc.vector.tensor_tensor(total[:], total[:], square[:], ADD)
+                    hs.append(h)
                 mean = mean_psum.tile([P, T], F32, name="mean")
                 nc.tensor.matmul(mean[:], mean_weights[:], total[:], start=True, stop=True)
                 r = norm.tile([P, T], F32, name="r")
@@ -97,7 +98,7 @@ def tile_repro_b_kernel(tc, emb, pos, gain, wq, bq, wk, bk, wv, bv, offs, out):
                 for k in range(KB):
                     x = norm.tile([P, T], BF16, name=f"x{k}")
                     nc.vector.scalar_tensor_tensor(
-                        x[:], hidden[k][:, span], gain_cols[k], r[:], MULT, MULT
+                        x[:], hs[k][:], gain_cols[k], r[:], MULT, MULT
                     )
                     xs.append(x)
                 return xs

@@ -1,5 +1,4 @@
 import concourse.mybir as mybir
-from concourse.masks import make_identity
 
 F32, BF16, U16 = mybir.dt.float32, mybir.dt.bfloat16, mybir.dt.uint16
 ADD, MULT = mybir.AluOpType.add, mybir.AluOpType.mult
@@ -11,6 +10,7 @@ EPS = 1.1920928955078125e-07
 KB = D // P
 MB = (D + HD + D) // P
 SEQS = N // T
+AHEAD = 3
 
 FLOPS = 2 * D * (D + HD + D) * N
 
@@ -19,28 +19,30 @@ def tile_repro_b_kernel(tc, emb, pos, gain, wq, bq, wk, bk, wv, bv, offs, out):
     nc = tc.nc
     with (
         tc.tile_pool(name="held", bufs=1) as held,
-        tc.tile_pool(name="hidden", bufs=3) as hidden,
-        tc.tile_pool(name="squares", bufs=8) as squares,
-        tc.tile_pool(name="sums", bufs=4) as sums,
+        tc.tile_pool(name="hidden", bufs=AHEAD) as hidden,
+        tc.tile_pool(name="squares", bufs=6) as squares,
+        tc.tile_pool(name="sums", bufs=AHEAD) as sums,
         tc.tile_pool(name="norm", bufs=3) as norm,
         tc.tile_pool(name="staged", bufs=8) as staged,
+        tc.psum_pool(name="mean_psum", bufs=2) as mean_psum,
+        tc.psum_pool(name="proj_psum", bufs=6) as proj_psum,
     ):
         offsets = held.tile([P, N // 16], U16, name="offsets")
         nc.sync.dma_start(offsets[:], offs)
 
-        vec_rows = held.tile([P, P], F32, name="vec_rows")
-        nc.vector.memset(vec_rows[:], 0.0)
-        first_row = 0
-        for vec in (gain, bq, bk, bv):
-            rows = vec.rearrange("(m p) o -> m (p o)", p=P)
-            nc.scalar.dma_start(vec_rows[first_row : first_row + rows.shape[0], :], rows)
-            first_row += rows.shape[0]
+        columns = []
+        for label, vec in (("gain", gain), ("bq", bq), ("bk", bk), ("bv", bv)):
+            cols = held.tile([P, vec.shape[0] // P], F32, name=label + "_cols")
+            nc.scalar.dma_start(cols[:], vec.rearrange("(a p) o -> p (a o)", p=P))
+            columns.append(cols)
+        gain_cols = [columns[0][:, k : k + 1] for k in range(KB)]
+        bias_cols = [cols[:, a : a + 1] for cols in columns[1:] for a in range(cols.shape[1])]
 
-        pos_sb = held.tile([P, KB, T], F32, name="pos_sb")
-        nc.sync.dma_start(pos_sb[:], pos.rearrange("(k p) t -> p k t", p=P))
-
-        tables = []
+        pos_blocks, tables = [], []
         for k in range(KB):
+            pos_block = held.tile([P, T], F32, name=f"pos{k}")
+            nc.sync.dma_start(pos_block[:], pos[k * P : (k + 1) * P, :])
+            pos_blocks.append(pos_block)
             table = held.tile([P, V], F32, name=f"table{k}")
             nc.sync.dma_start(table[:], emb[k * P : (k + 1) * P, :])
             tables.append(table)
@@ -59,69 +61,58 @@ def tile_repro_b_kernel(tc, emb, pos, gain, wq, bq, wk, bk, wv, bv, offs, out):
         eps_col = held.tile([P, 1], F32, name="eps_col")
         nc.vector.memset(eps_col[:], EPS)
 
-        identity = held.tile([P, P], F32, name="identity")
-        make_identity(nc, identity[:])
-        vec_cols = held.tile([P, KB + MB], F32, name="vec_cols")
-        with tc.psum_pool(name="setup_psum", bufs=1) as setup_psum:
-            flipped = setup_psum.tile([P, P], F32, name="flipped")
-            nc.tensor.transpose(flipped[:], vec_rows[:], identity[:])
-            nc.vector.tensor_copy(vec_cols[:], flipped[:, 0 : KB + MB])
-        gain_cols = [vec_cols[:, k : k + 1] for k in range(KB)]
-        bias_cols = [vec_cols[:, KB + m : KB + m + 1] for m in range(MB)]
+        def look_up(s):
+            span = slice(s * T, (s + 1) * T)
+            piece = offsets[:, s * (T // 16) : (s + 1) * (T // 16)]
+            total = sums.tile([P, T], F32, name="total")
+            h = hidden.tile([P, KB, T], F32, name="h")
+            for k in range(KB):
+                nc.vector.tensor_tensor(
+                    h[:, k, :], tables[k][:].indirect(piece), pos_blocks[k][:], ADD
+                )
+                if k == 0:
+                    nc.scalar.activation(total[:], h[:, k, :], ACT.Square)
+                else:
+                    square = squares.tile([P, T], F32, name="square")
+                    nc.scalar.activation(square[:], h[:, k, :], ACT.Square)
+                    nc.vector.tensor_tensor(total[:], total[:], square[:], ADD)
+            nc.sync.dma_start(out[0:D, span].rearrange("(k p) t -> p k t", p=P), h[:])
+            return h, total
 
-        with (
-            tc.psum_pool(name="mean_psum", bufs=2) as mean_psum,
-            tc.psum_pool(name="proj_psum", bufs=6) as proj_psum,
-        ):
+        def normalize(h, total):
+            mean = mean_psum.tile([P, T], F32, name="mean")
+            nc.tensor.matmul(mean[:], mean_weights[:], total[:], start=True, stop=True)
+            r = norm.tile([P, T], F32, name="r")
+            nc.scalar.activation(r[:], mean[:], ACT.Abs_reciprocal_sqrt, bias=eps_col[:])
+            xs = []
+            for k in range(KB):
+                x = norm.tile([P, T], BF16, name=f"x{k}")
+                nc.vector.scalar_tensor_tensor(x[:], h[:, k, :], gain_cols[k], r[:], MULT, MULT)
+                xs.append(x)
+            return xs
 
-            def normalize(s):
-                span = slice(s * T, (s + 1) * T)
-                piece = offsets[:, s * (T // 16) : (s + 1) * (T // 16)]
-                total = sums.tile([P, T], F32, name="total")
-                hs = []
+        def project(s, xs):
+            span = slice(s * T, (s + 1) * T)
+            for m in range(MB):
+                acc = proj_psum.tile([P, T], F32, name="acc")
                 for k in range(KB):
-                    h = hidden.tile([P, T], F32, name=f"h{k}")
-                    nc.vector.tensor_tensor(h[:], tables[k][:].indirect(piece), pos_sb[:, k, :], ADD)
-                    nc.sync.dma_start(out[k * P : (k + 1) * P, span], h[:])
-                    if k == 0:
-                        nc.scalar.activation(total[:], h[:], ACT.Square)
-                    else:
-                        square = squares.tile([P, T], F32, name="square")
-                        nc.scalar.activation(square[:], h[:], ACT.Square)
-                        nc.vector.tensor_tensor(total[:], total[:], square[:], ADD)
-                    hs.append(h)
-                mean = mean_psum.tile([P, T], F32, name="mean")
-                nc.tensor.matmul(mean[:], mean_weights[:], total[:], start=True, stop=True)
-                r = norm.tile([P, T], F32, name="r")
-                nc.scalar.activation(r[:], mean[:], ACT.Abs_reciprocal_sqrt, bias=eps_col[:])
-                xs = []
-                for k in range(KB):
-                    x = norm.tile([P, T], BF16, name=f"x{k}")
-                    nc.vector.scalar_tensor_tensor(
-                        x[:], hs[k][:], gain_cols[k], r[:], MULT, MULT
+                    nc.tensor.matmul(
+                        acc[:],
+                        weights[:, k, m * P : (m + 1) * P],
+                        xs[k][:],
+                        start=(k == 0),
+                        stop=(k == KB - 1),
                     )
-                    xs.append(x)
-                return xs
+                y = staged.tile([P, T], F32, name="y")
+                nc.scalar.activation(y[:], acc[:], ACT.Identity, bias=bias_cols[m])
+                nc.sync.dma_start(out[D + m * P : D + (m + 1) * P, span], y[:])
 
-            def project(s, xs):
-                span = slice(s * T, (s + 1) * T)
-                for m in range(MB):
-                    acc = proj_psum.tile([P, T], F32, name="acc")
-                    for k in range(KB):
-                        nc.tensor.matmul(
-                            acc[:],
-                            weights[:, k, m * P : (m + 1) * P],
-                            xs[k][:],
-                            start=(k == 0),
-                            stop=(k == KB - 1),
-                        )
-                    y = staged.tile([P, T], F32, name="y")
-                    nc.scalar.activation(y[:], acc[:], ACT.Identity, bias=bias_cols[m])
-                    nc.sync.dma_start(out[D + m * P : D + (m + 1) * P, span], y[:])
-
-            xs_next = normalize(0)
-            for s in range(SEQS):
-                xs_now = xs_next
-                if s + 1 < SEQS:
-                    xs_next = normalize(s + 1)
-                project(s, xs_now)
+        looked_up = [look_up(s) for s in range(AHEAD)]
+        xs_next = normalize(*looked_up[0])
+        for s in range(SEQS):
+            xs_now = xs_next
+            if s + AHEAD < SEQS:
+                looked_up.append(look_up(s + AHEAD))
+            if s + 1 < SEQS:
+                xs_next = normalize(*looked_up[s + 1])
+            project(s, xs_now)

@@ -10,7 +10,8 @@ EPS = 1.1920928955078125e-07
 KB = D // P
 MB = (D + HD + D) // P
 SEQS = N // T
-AHEAD = 3
+PIECES = [(0, 0, T // 4), (0, T // 4, T // 4), (0, T // 2, T // 2)] + [(s, 0, T) for s in range(1, SEQS)]
+H_TILES = 3
 
 FLOPS = 2 * D * (D + HD + D) * N
 
@@ -19,100 +20,109 @@ def tile_repro_b_kernel(tc, emb, pos, gain, wq, bq, wk, bk, wv, bv, offs, out):
     nc = tc.nc
     with (
         tc.tile_pool(name="held", bufs=1) as held,
-        tc.tile_pool(name="hidden", bufs=AHEAD) as hidden,
+        tc.tile_pool(name="hidden", bufs=H_TILES) as hidden,
         tc.tile_pool(name="squares", bufs=6) as squares,
-        tc.tile_pool(name="sums", bufs=AHEAD) as sums,
+        tc.tile_pool(name="sums", bufs=5) as sums,
         tc.tile_pool(name="norm", bufs=3) as norm,
-        tc.tile_pool(name="staged", bufs=8) as staged,
-        tc.psum_pool(name="mean_psum", bufs=2) as mean_psum,
-        tc.psum_pool(name="proj_psum", bufs=6) as proj_psum,
+        tc.tile_pool(name="staged", bufs=2) as staged,
+        tc.psum_pool(name="psum", bufs=8) as psum,
     ):
         offsets = held.tile([P, N // 16], U16, name="offsets")
         nc.sync.dma_start(offsets[:], offs)
 
-        columns = []
-        for label, vec in (("gain", gain), ("bq", bq), ("bk", bk), ("bv", bv)):
+        gains = held.tile([P, KB], F32, name="gains")
+        nc.scalar.dma_start(gains[:], gain.rearrange("(p k) o -> p (k o)", k=KB))
+        gain_cols = [gains[:, k : k + 1] for k in range(KB)]
+        bias_cols = []
+        for label, vec in (("bq", bq), ("bk", bk), ("bv", bv)):
             cols = held.tile([P, vec.shape[0] // P], F32, name=label + "_cols")
             nc.scalar.dma_start(cols[:], vec.rearrange("(a p) o -> p (a o)", p=P))
-            columns.append(cols)
-        gain_cols = [columns[0][:, k : k + 1] for k in range(KB)]
-        bias_cols = [cols[:, a : a + 1] for cols in columns[1:] for a in range(cols.shape[1])]
+            bias_cols.extend([cols[:, a : a + 1] for a in range(cols.shape[1])])
 
         pos_blocks, tables = [], []
         for k in range(KB):
             pos_block = held.tile([P, T], F32, name=f"pos{k}")
-            nc.sync.dma_start(pos_block[:], pos[k * P : (k + 1) * P, :])
+            nc.sync.dma_start(pos_block[:], pos.rearrange("(p k) t -> k p t", k=KB)[k])
             pos_blocks.append(pos_block)
             table = held.tile([P, V], F32, name=f"table{k}")
-            nc.sync.dma_start(table[:], emb[k * P : (k + 1) * P, :])
+            nc.sync.dma_start(table[:], emb.rearrange("(p k) v -> k p v", k=KB)[k])
             tables.append(table)
 
-        weights = held.tile([P, KB, MB * P], BF16, name="weights")
-        first_col = 0
-        for w in (wq, wk, wv):
-            cols = w.shape[1]
-            nc.sync.dma_start(
-                weights[:, :, first_col : first_col + cols], w.rearrange("(k p) m -> p k m", p=P)
-            )
-            first_col += cols
+        weight_blocks = []
+        for label, w in (("wq", wq), ("wk", wk), ("wv", wv)):
+            w_sb = held.tile([P, KB, w.shape[1]], BF16, name=label + "_sb")
+            nc.sync.dma_start(w_sb[:], w.rearrange("(p k) m -> p k m", k=KB))
+            weight_blocks.extend([w_sb[:, :, a * P : (a + 1) * P] for a in range(w.shape[1] // P)])
 
         mean_weights = held.tile([P, P], F32, name="mean_weights")
         nc.vector.memset(mean_weights[:], 1.0 / D)
         eps_col = held.tile([P, 1], F32, name="eps_col")
         nc.vector.memset(eps_col[:], EPS)
 
-        def look_up(s):
-            span = slice(s * T, (s + 1) * T)
-            piece = offsets[:, s * (T // 16) : (s + 1) * (T // 16)]
-            total = sums.tile([P, T], F32, name="total")
-            h = hidden.tile([P, KB, T], F32, name="h")
+        h_tiles, y_tiles = [], []
+
+        def look_up(i):
+            s, first, width = PIECES[i]
+            places = slice(first, first + width)
+            piece = offsets[:, (s * T + first) // 16 : (s * T + first + width) // 16]
+            if first == 0:
+                h_tiles.append(hidden.tile([P, KB, T], F32, name="h_seq"))
+            h = h_tiles[s][:, :, places]
+            total = sums.tile([P, width], F32, name="total")
             for k in range(KB):
                 nc.vector.tensor_tensor(
-                    h[:, k, :], tables[k][:].indirect(piece), pos_blocks[k][:], ADD
+                    h[:, k, :], tables[k][:].indirect(piece), pos_blocks[k][:, places], ADD
                 )
                 if k == 0:
                     nc.scalar.activation(total[:], h[:, k, :], ACT.Square)
                 else:
-                    square = squares.tile([P, T], F32, name="square")
+                    square = squares.tile([P, width], F32, name="square")
                     nc.scalar.activation(square[:], h[:, k, :], ACT.Square)
                     nc.vector.tensor_tensor(total[:], total[:], square[:], ADD)
-            nc.sync.dma_start(out[0:D, span].rearrange("(k p) t -> p k t", p=P), h[:])
+            if first + width == T:
+                nc.sync.dma_start(
+                    out[0:D, s * T : (s + 1) * T].rearrange("(p k) t -> p k t", k=KB), h_tiles[s][:]
+                )
             return h, total
 
         def normalize(h, total):
-            mean = mean_psum.tile([P, T], F32, name="mean")
+            width = total.shape[1]
+            mean = psum.tile([P, width], F32, name="mean", tag="bank")
             nc.tensor.matmul(mean[:], mean_weights[:], total[:], start=True, stop=True)
-            r = norm.tile([P, T], F32, name="r")
+            r = norm.tile([P, width], F32, name="r")
             nc.scalar.activation(r[:], mean[:], ACT.Abs_reciprocal_sqrt, bias=eps_col[:])
             xs = []
             for k in range(KB):
-                x = norm.tile([P, T], BF16, name=f"x{k}")
+                x = norm.tile([P, width], BF16, name=f"x{k}")
                 nc.vector.scalar_tensor_tensor(x[:], h[:, k, :], gain_cols[k], r[:], MULT, MULT)
                 xs.append(x)
             return xs
 
-        def project(s, xs):
-            span = slice(s * T, (s + 1) * T)
+        def project(i, xs):
+            s, first, width = PIECES[i]
+            if first == 0:
+                y_tiles.append(staged.tile([P, MB, T], F32, name="y_seq"))
             for m in range(MB):
-                acc = proj_psum.tile([P, T], F32, name="acc")
+                acc = psum.tile([P, width], F32, name="acc", tag="bank")
                 for k in range(KB):
                     nc.tensor.matmul(
                         acc[:],
-                        weights[:, k, m * P : (m + 1) * P],
+                        weight_blocks[m][:, k, :],
                         xs[k][:],
                         start=(k == 0),
                         stop=(k == KB - 1),
                     )
-                y = staged.tile([P, T], F32, name="y")
-                nc.scalar.activation(y[:], acc[:], ACT.Identity, bias=bias_cols[m])
-                nc.sync.dma_start(out[D + m * P : D + (m + 1) * P, span], y[:])
+                y = y_tiles[s][:, m, :]
+                nc.scalar.activation(
+                    y[:, first : first + width], acc[:], ACT.Identity, bias=bias_cols[m]
+                )
+                if first + width == T:
+                    nc.sync.dma_start(out[D + m * P : D + (m + 1) * P, s * T : (s + 1) * T], y)
 
-        looked_up = [look_up(s) for s in range(AHEAD)]
-        xs_next = normalize(*looked_up[0])
-        for s in range(SEQS):
+        pieces = len(PIECES)
+        xs_next = normalize(*look_up(0))
+        for i in range(pieces):
             xs_now = xs_next
-            if s + AHEAD < SEQS:
-                looked_up.append(look_up(s + AHEAD))
-            if s + 1 < SEQS:
-                xs_next = normalize(*looked_up[s + 1])
-            project(s, xs_now)
+            if i + 1 < pieces:
+                xs_next = normalize(*look_up(i + 1))
+            project(i, xs_now)

@@ -10,8 +10,7 @@ EPS = 1.1920928955078125e-07
 KB = D // P
 MB = (D + HD + D) // P
 SEQS = N // T
-PIECES = [(0, 0, T // 4), (0, T // 4, T // 4), (0, T // 2, T // 2)] + [(s, 0, T) for s in range(1, SEQS)]
-H_TILES = 3
+EARLY = 3
 
 FLOPS = 2 * D * (D + HD + D) * N
 
@@ -20,9 +19,8 @@ def tile_repro_b_kernel(tc, emb, pos, gain, wq, bq, wk, bk, wv, bv, offs, out):
     nc = tc.nc
     with (
         tc.tile_pool(name="held", bufs=1) as held,
-        tc.tile_pool(name="hidden", bufs=H_TILES) as hidden,
-        tc.tile_pool(name="squares", bufs=6) as squares,
-        tc.tile_pool(name="sums", bufs=5) as sums,
+        tc.tile_pool(name="hidden", bufs=EARLY) as hidden,
+        tc.tile_pool(name="squares", bufs=8) as squares,
         tc.tile_pool(name="norm", bufs=3) as norm,
         tc.tile_pool(name="staged", bufs=2) as staged,
         tc.psum_pool(name="psum", bufs=8) as psum,
@@ -59,70 +57,66 @@ def tile_repro_b_kernel(tc, emb, pos, gain, wq, bq, wk, bk, wv, bv, offs, out):
         eps_col = held.tile([P, 1], F32, name="eps_col")
         nc.vector.memset(eps_col[:], EPS)
 
-        h_tiles, y_tiles = [], []
+        h_tiles, means = [], []
 
-        def look_up(i):
-            s, first, width = PIECES[i]
-            places = slice(first, first + width)
-            piece = offsets[:, (s * T + first) // 16 : (s * T + first + width) // 16]
-            if first == 0:
-                h_tiles.append(hidden.tile([P, KB, T], F32, name="h_seq"))
-            h = h_tiles[s][:, :, places]
-            total = sums.tile([P, width], F32, name="total")
-            for k in range(KB):
-                nc.vector.tensor_tensor(
-                    h[:, k, :], tables[k][:].indirect(piece), pos_blocks[k][:, places], ADD
-                )
-                if k == 0:
-                    nc.scalar.activation(total[:], h[:, k, :], ACT.Square)
-                else:
-                    square = squares.tile([P, width], F32, name="square")
-                    nc.scalar.activation(square[:], h[:, k, :], ACT.Square)
+        def open_sequence():
+            h_tiles.append(hidden.tile([P, KB, T], F32, name="h"))
+            means.append(psum.tile([P, T], F32, name="mean", tag="bank"))
+
+        def look_up(s, k):
+            h = h_tiles[s][:, k, :]
+            piece = offsets[:, s * (T // 16) : (s + 1) * (T // 16)]
+            nc.vector.tensor_tensor(h, tables[k][:].indirect(piece), pos_blocks[k][:], ADD)
+            square = squares.tile([P, T], F32, name="square")
+            nc.scalar.activation(square[:], h, ACT.Square)
+            return square
+
+        def normalize(s):
+            if s < EARLY:
+                square = look_up(s, KB - 1)
+                nc.tensor.matmul(means[s][:], mean_weights[:], square[:], start=False, stop=True)
+            else:
+                open_sequence()
+                total = look_up(s, 0)
+                for k in range(1, KB):
+                    square = look_up(s, k)
                     nc.vector.tensor_tensor(total[:], total[:], square[:], ADD)
-            if first + width == T:
-                nc.sync.dma_start(
-                    out[0:D, s * T : (s + 1) * T].rearrange("(p k) t -> p k t", k=KB), h_tiles[s][:]
-                )
-            return h, total
-
-        def normalize(h, total):
-            width = total.shape[1]
-            mean = psum.tile([P, width], F32, name="mean", tag="bank")
-            nc.tensor.matmul(mean[:], mean_weights[:], total[:], start=True, stop=True)
-            r = norm.tile([P, width], F32, name="r")
-            nc.scalar.activation(r[:], mean[:], ACT.Abs_reciprocal_sqrt, bias=eps_col[:])
+                nc.tensor.matmul(means[s][:], mean_weights[:], total[:], start=True, stop=True)
+            nc.sync.dma_start(
+                out[0:D, s * T : (s + 1) * T].rearrange("(p k) t -> p k t", k=KB), h_tiles[s][:]
+            )
+            r = norm.tile([P, T], F32, name="r")
+            nc.scalar.activation(r[:], means[s][:], ACT.Abs_reciprocal_sqrt, bias=eps_col[:])
             xs = []
             for k in range(KB):
-                x = norm.tile([P, width], BF16, name=f"x{k}")
-                nc.vector.scalar_tensor_tensor(x[:], h[:, k, :], gain_cols[k], r[:], MULT, MULT)
+                x = norm.tile([P, T], BF16, name=f"x{k}")
+                nc.vector.scalar_tensor_tensor(
+                    x[:], h_tiles[s][:, k, :], gain_cols[k], r[:], MULT, MULT
+                )
                 xs.append(x)
             return xs
 
-        def project(i, xs):
-            s, first, width = PIECES[i]
-            if first == 0:
-                y_tiles.append(staged.tile([P, MB, T], F32, name="y_seq"))
+        def project(s, xs):
+            y = staged.tile([P, MB, T], F32, name="y")
             for m in range(MB):
-                acc = psum.tile([P, width], F32, name="acc", tag="bank")
+                acc = psum.tile([P, T], F32, name="acc", tag="bank")
                 for k in range(KB):
                     nc.tensor.matmul(
-                        acc[:],
-                        weight_blocks[m][:, k, :],
-                        xs[k][:],
-                        start=(k == 0),
-                        stop=(k == KB - 1),
+                        acc[:], weight_blocks[m][:, k, :], xs[k][:], start=(k == 0), stop=(k == KB - 1)
                     )
-                y = y_tiles[s][:, m, :]
-                nc.scalar.activation(
-                    y[:, first : first + width], acc[:], ACT.Identity, bias=bias_cols[m]
-                )
-                if first + width == T:
-                    nc.sync.dma_start(out[D + m * P : D + (m + 1) * P, s * T : (s + 1) * T], y)
+                nc.scalar.activation(y[:, m, :], acc[:], ACT.Identity, bias=bias_cols[m])
+                nc.sync.dma_start(out[D + m * P : D + (m + 1) * P, s * T : (s + 1) * T], y[:, m, :])
 
-        pieces = len(PIECES)
-        xs_next = normalize(*look_up(0))
-        for i in range(pieces):
+        for s in range(EARLY):
+            open_sequence()
+        for k in range(KB - 1):
+            for s in range(EARLY):
+                square = look_up(s, k)
+                nc.tensor.matmul(means[s][:], mean_weights[:], square[:], start=(k == 0), stop=False)
+
+        xs_next = normalize(0)
+        for s in range(SEQS):
             xs_now = xs_next
-            if i + 1 < pieces:
-                xs_next = normalize(*look_up(i + 1))
-            project(i, xs_now)
+            if s + 1 < SEQS:
+                xs_next = normalize(s + 1)
+            project(s, xs_now)

@@ -28,15 +28,6 @@ def tile_repro_b_kernel(tc, emb, pos, gain, wq, bq, wk, bk, wv, bv, offs, out):
         offsets = held.tile([P, N // 16], U16, name="offsets")
         nc.sync.dma_start(offsets[:], offs)
 
-        gains = held.tile([P, KB], F32, name="gains")
-        nc.scalar.dma_start(gains[:], gain.rearrange("(p k) o -> p (k o)", k=KB))
-        gain_cols = [gains[:, k : k + 1] for k in range(KB)]
-        bias_cols = []
-        for label, vec in (("bq", bq), ("bk", bk), ("bv", bv)):
-            cols = held.tile([P, vec.shape[0] // P], F32, name=label + "_cols")
-            nc.scalar.dma_start(cols[:], vec.rearrange("(a p) o -> p (a o)", p=P))
-            bias_cols.extend([cols[:, a : a + 1] for a in range(cols.shape[1])])
-
         pos_blocks, tables = [], []
         for k in range(KB):
             pos_block = held.tile([P, T], F32, name=f"pos{k}")
@@ -46,11 +37,21 @@ def tile_repro_b_kernel(tc, emb, pos, gain, wq, bq, wk, bk, wv, bv, offs, out):
             nc.sync.dma_start(table[:], emb.rearrange("(p k) v -> k p v", k=KB)[k])
             tables.append(table)
 
+        gains = held.tile([P, KB], F32, name="gains")
+        nc.sync.dma_start(gains[:], gain.rearrange("(p k) o -> p (k o)", k=KB))
+        gain_cols = [gains[:, k : k + 1] for k in range(KB)]
+
         weight_blocks = []
         for label, w in (("wq", wq), ("wk", wk), ("wv", wv)):
             w_sb = held.tile([P, KB, w.shape[1]], BF16, name=label + "_sb")
             nc.sync.dma_start(w_sb[:], w.rearrange("(p k) m -> p k m", k=KB))
             weight_blocks.extend([w_sb[:, :, a * P : (a + 1) * P] for a in range(w.shape[1] // P)])
+
+        bias_cols = []
+        for label, vec in (("bq", bq), ("bk", bk), ("bv", bv)):
+            cols = held.tile([P, vec.shape[0] // P], F32, name=label + "_cols")
+            nc.sync.dma_start(cols[:], vec.rearrange("(a p) o -> p (a o)", p=P))
+            bias_cols.extend([cols[:, a : a + 1] for a in range(cols.shape[1])])
 
         mean_weights = held.tile([P, P], F32, name="mean_weights")
         nc.vector.memset(mean_weights[:], 1.0 / D)

@@ -1,7 +1,8 @@
 import concourse.mybir as mybir
 
 F32, BF16, U16 = mybir.dt.float32, mybir.dt.bfloat16, mybir.dt.uint16
-ADD, MULT = mybir.AluOpType.add, mybir.AluOpType.mult
+ADD, MULT, NOT_EQUAL = mybir.AluOpType.add, mybir.AluOpType.mult, mybir.AluOpType.not_equal
+X_AXIS = mybir.AxisListType.X
 ACT = mybir.ActivationFunctionType
 
 P = 128
@@ -10,6 +11,7 @@ EPS = 1.1920928955078125e-07
 KB = D // P
 MB = (D + HD + D) // P
 SEQS = N // T
+QUAD = 32
 EARLY = 3
 
 FLOPS = 2 * D * (D + HD + D) * N
@@ -22,6 +24,7 @@ def tile_repro_b_kernel(tc, emb, pos, gain, wq, bq, wk, bk, wv, bv, offs, out):
         tc.tile_pool(name="hidden", bufs=EARLY) as hidden,
         tc.tile_pool(name="squares", bufs=8) as squares,
         tc.tile_pool(name="norm", bufs=3) as norm,
+        tc.tile_pool(name="turn", bufs=2) as turn,
         tc.tile_pool(name="staged", bufs=2) as staged,
         tc.psum_pool(name="psum", bufs=8) as psum,
     ):
@@ -55,20 +58,47 @@ def tile_repro_b_kernel(tc, emb, pos, gain, wq, bq, wk, bk, wv, bv, offs, out):
 
         mean_weights = held.tile([P, P], F32, name="mean_weights")
         nc.vector.memset(mean_weights[:], 1.0 / D)
+        quad_weights = held.tile([P, P], F32, name="quad_weights")
+        nc.gpsimd.memset(quad_weights[:], 0.0)
+        for shift in range(QUAD - P, P, QUAD):
+            nc.gpsimd.affine_select(
+                out=quad_weights[:],
+                in_=quad_weights[:],
+                pattern=[[-1, P]],
+                compare_op=NOT_EQUAL,
+                fill=1.0 / D,
+                base=shift,
+                channel_multiplier=1,
+            )
         eps_col = held.tile([P, 1], F32, name="eps_col")
         nc.vector.memset(eps_col[:], EPS)
 
         h_tiles, means = [], []
 
-        def open_sequence():
-            h_tiles.append(hidden.tile([P, KB, T], F32, name="h"))
-            means.append(psum.tile([P, T], F32, name="mean", tag="bank"))
+        def root_of_mean(total):
+            turned = turn.tile([P, T], F32, name="turned", align_bytes=64)
+            nc.vector.transpose(turned[:], total[:])
+            part = turn.tile([P, T // QUAD], F32, name="part")
+            nc.vector.tensor_reduce(part[:], turned[:].rearrange("p (b i) -> p b i", i=QUAD), X_AXIS, ADD)
+            mean = psum.tile([P, T // QUAD], F32, name="narrow", tag="bank")
+            nc.tensor.matmul(mean[:], quad_weights[:], part[:], start=True, stop=True)
+            spread = turn.tile([P, T // QUAD, QUAD], F32, name="spread", align_bytes=64)
+            nc.scalar.activation(
+                spread[:],
+                mean[:].unsqueeze(2).to_broadcast([P, T // QUAD, QUAD]),
+                ACT.Abs_reciprocal_sqrt,
+                bias=eps_col[:],
+            )
+            r = norm.tile([P, T], F32, name="r", align_bytes=64)
+            nc.vector.transpose(r[:], spread[:].rearrange("p b i -> p (b i)"))
+            return r
+
 
         def look_up(s, k):
             h = h_tiles[s][:, k, :]
             piece = offsets[:, s * (T // 16) : (s + 1) * (T // 16)]
             nc.vector.tensor_tensor(h, tables[k][:].indirect(piece), pos_blocks[k][:], ADD)
-            square = squares.tile([P, T], F32, name="square")
+            square = squares.tile([P, T], F32, name="square", align_bytes=64)
             nc.scalar.activation(square[:], h, ACT.Square)
             return square
 
@@ -76,18 +106,18 @@ def tile_repro_b_kernel(tc, emb, pos, gain, wq, bq, wk, bk, wv, bv, offs, out):
             if s < EARLY:
                 square = look_up(s, KB - 1)
                 nc.tensor.matmul(means[s][:], mean_weights[:], square[:], start=False, stop=True)
+                r = norm.tile([P, T], F32, name="r", align_bytes=64)
+                nc.scalar.activation(r[:], means[s][:], ACT.Abs_reciprocal_sqrt, bias=eps_col[:])
             else:
-                open_sequence()
+                h_tiles.append(hidden.tile([P, KB, T], F32, name="h"))
                 total = look_up(s, 0)
                 for k in range(1, KB):
                     square = look_up(s, k)
                     nc.vector.tensor_tensor(total[:], total[:], square[:], ADD)
-                nc.tensor.matmul(means[s][:], mean_weights[:], total[:], start=True, stop=True)
+                r = root_of_mean(total)
             nc.sync.dma_start(
                 out[0:D, s * T : (s + 1) * T].rearrange("(p k) t -> p k t", k=KB), h_tiles[s][:]
             )
-            r = norm.tile([P, T], F32, name="r")
-            nc.scalar.activation(r[:], means[s][:], ACT.Abs_reciprocal_sqrt, bias=eps_col[:])
             xs = []
             for k in range(KB):
                 x = norm.tile([P, T], BF16, name=f"x{k}")
@@ -109,7 +139,8 @@ def tile_repro_b_kernel(tc, emb, pos, gain, wq, bq, wk, bk, wv, bv, offs, out):
                 nc.sync.dma_start(out[D + m * P : D + (m + 1) * P, s * T : (s + 1) * T], y[:, m, :])
 
         for s in range(EARLY):
-            open_sequence()
+            h_tiles.append(hidden.tile([P, KB, T], F32, name="h"))
+            means.append(psum.tile([P, T], F32, name="mean", tag="bank"))
         for k in range(KB - 1):
             for s in range(EARLY):
                 square = look_up(s, k)

@@ -13,6 +13,7 @@ MB = (D + HD + D) // P
 SEQS = N // T
 QUAD = 32
 EARLY = 3
+LATE = 5
 
 FLOPS = 2 * D * (D + HD + D) * N
 
@@ -75,7 +76,12 @@ def tile_repro_b_kernel(tc, emb, pos, gain, wq, bq, wk, bk, wv, bv, offs, out):
 
         h_tiles, means = [], []
 
-        def root_of_mean(total):
+        def root(mean):
+            r = norm.tile([P, T], F32, name="r", align_bytes=64)
+            nc.scalar.activation(r[:], mean[:], ACT.Abs_reciprocal_sqrt, bias=eps_col[:])
+            return r
+
+        def root_by_transposes(total):
             turned = turn.tile([P, T], F32, name="turned", align_bytes=64)
             nc.vector.transpose(turned[:], total[:])
             part = turn.tile([P, T // QUAD], F32, name="part")
@@ -93,7 +99,6 @@ def tile_repro_b_kernel(tc, emb, pos, gain, wq, bq, wk, bk, wv, bv, offs, out):
             nc.vector.transpose(r[:], spread[:].rearrange("p b i -> p (b i)"))
             return r
 
-
         def look_up(s, k):
             h = h_tiles[s][:, k, :]
             piece = offsets[:, s * (T // 16) : (s + 1) * (T // 16)]
@@ -106,15 +111,19 @@ def tile_repro_b_kernel(tc, emb, pos, gain, wq, bq, wk, bk, wv, bv, offs, out):
             if s < EARLY:
                 square = look_up(s, KB - 1)
                 nc.tensor.matmul(means[s][:], mean_weights[:], square[:], start=False, stop=True)
-                r = norm.tile([P, T], F32, name="r", align_bytes=64)
-                nc.scalar.activation(r[:], means[s][:], ACT.Abs_reciprocal_sqrt, bias=eps_col[:])
+                r = root(means[s])
             else:
                 h_tiles.append(hidden.tile([P, KB, T], F32, name="h"))
                 total = look_up(s, 0)
                 for k in range(1, KB):
                     square = look_up(s, k)
                     nc.vector.tensor_tensor(total[:], total[:], square[:], ADD)
-                r = root_of_mean(total)
+                if s < LATE:
+                    mean = psum.tile([P, T], F32, name="mean", tag="bank")
+                    nc.tensor.matmul(mean[:], mean_weights[:], total[:], start=True, stop=True)
+                    r = root(mean)
+                else:
+                    r = root_by_transposes(total)
             nc.sync.dma_start(
                 out[0:D, s * T : (s + 1) * T].rearrange("(p k) t -> p k t", k=KB), h_tiles[s][:]
             )

@@ -12,8 +12,9 @@ KB = D // P
 MB = (D + HD + D) // P
 SEQS = N // T
 QUAD = 32
+HALF = T // 2
 EARLY = 3
-LATE = 5
+LATE = 6
 
 FLOPS = 2 * D * (D + HD + D) * N
 
@@ -25,6 +26,7 @@ def tile_repro_b_kernel(tc, emb, pos, gain, wq, bq, wk, bk, wv, bv, offs, out):
         tc.tile_pool(name="hidden", bufs=EARLY) as hidden,
         tc.tile_pool(name="squares", bufs=8) as squares,
         tc.tile_pool(name="norm", bufs=3) as norm,
+        tc.tile_pool(name="four", bufs=1) as four,
         tc.tile_pool(name="turn", bufs=2) as turn,
         tc.tile_pool(name="staged", bufs=2) as staged,
         tc.psum_pool(name="psum", bufs=8) as psum,
@@ -32,14 +34,18 @@ def tile_repro_b_kernel(tc, emb, pos, gain, wq, bq, wk, bk, wv, bv, offs, out):
         offsets = held.tile([P, N // 16], U16, name="offsets")
         nc.sync.dma_start(offsets[:], offs)
 
+        pos_rows = pos.rearrange("(p k) t -> k p t", k=KB)
+        emb_rows = emb.rearrange("(p k) v -> k p v", k=KB)
         pos_blocks, tables = [], []
         for k in range(KB):
             pos_block = held.tile([P, T], F32, name=f"pos{k}")
-            nc.sync.dma_start(pos_block[:], pos.rearrange("(p k) t -> k p t", k=KB)[k])
+            ahead = T if k < KB - 1 else HALF
+            nc.sync.dma_start(pos_block[:, 0:ahead], pos_rows[k][:, 0:ahead])
             pos_blocks.append(pos_block)
             table = held.tile([P, V], F32, name=f"table{k}")
-            nc.sync.dma_start(table[:], emb.rearrange("(p k) v -> k p v", k=KB)[k])
+            nc.sync.dma_start(table[:], emb_rows[k])
             tables.append(table)
+        nc.sync.dma_start(pos_blocks[KB - 1][:, HALF:T], pos_rows[KB - 1][:, HALF:T])
 
         gains = held.tile([P, KB], F32, name="gains")
         nc.sync.dma_start(gains[:], gain.rearrange("(p k) o -> p (k o)", k=KB))
@@ -74,90 +80,121 @@ def tile_repro_b_kernel(tc, emb, pos, gain, wq, bq, wk, bk, wv, bv, offs, out):
         eps_col = held.tile([P, 1], F32, name="eps_col")
         nc.vector.memset(eps_col[:], EPS)
 
-        h_tiles, means = [], []
+        whole = slice(0, T)
 
-        def root(mean):
-            r = norm.tile([P, T], F32, name="r", align_bytes=64)
-            nc.scalar.activation(r[:], mean[:], ACT.Abs_reciprocal_sqrt, bias=eps_col[:])
+        def pieces_of(s):
+            return [slice(0, HALF), slice(HALF, T)] if s == 0 else [whole]
+
+        h_tiles, means = [], {}
+
+        def look_up(s, k, cols, square):
+            h = h_tiles[s][:, k, cols]
+            piece = offsets[:, (s * T + cols.start) // 16 : (s * T + cols.stop) // 16]
+            nc.vector.tensor_tensor(h, tables[k][:].indirect(piece), pos_blocks[k][:, cols], ADD)
+            nc.scalar.activation(square, h, ACT.Square)
+
+        def root(mean, cols):
+            width = cols.stop - cols.start
+            r = norm.tile([P, width], F32, name="r", tag=f"r{width}", align_bytes=64)
+            nc.scalar.activation(r[:], mean[:, cols], ACT.Abs_reciprocal_sqrt, bias=eps_col[:])
             return r
 
         def root_by_transposes(total):
             turned = turn.tile([P, T], F32, name="turned", align_bytes=64)
-            nc.vector.transpose(turned[:], total[:])
+            nc.vector.transpose(turned[:], total)
             part = turn.tile([P, T // QUAD], F32, name="part")
             nc.vector.tensor_reduce(part[:], turned[:].rearrange("p (b i) -> p b i", i=QUAD), X_AXIS, ADD)
-            mean = psum.tile([P, T // QUAD], F32, name="narrow", tag="bank")
-            nc.tensor.matmul(mean[:], quad_weights[:], part[:], start=True, stop=True)
+            narrow = psum.tile([P, T // QUAD], F32, name="narrow", tag="bank")
+            nc.tensor.matmul(narrow[:], quad_weights[:], part[:], start=True, stop=True)
             spread = turn.tile([P, T // QUAD, QUAD], F32, name="spread", align_bytes=64)
             nc.scalar.activation(
                 spread[:],
-                mean[:].unsqueeze(2).to_broadcast([P, T // QUAD, QUAD]),
+                narrow[:].unsqueeze(2).to_broadcast([P, T // QUAD, QUAD]),
                 ACT.Abs_reciprocal_sqrt,
                 bias=eps_col[:],
             )
-            r = norm.tile([P, T], F32, name="r", align_bytes=64)
+            r = norm.tile([P, T], F32, name="r", tag=f"r{T}", align_bytes=64)
             nc.vector.transpose(r[:], spread[:].rearrange("p b i -> p (b i)"))
             return r
 
-        def look_up(s, k):
-            h = h_tiles[s][:, k, :]
-            piece = offsets[:, s * (T // 16) : (s + 1) * (T // 16)]
-            nc.vector.tensor_tensor(h, tables[k][:].indirect(piece), pos_blocks[k][:], ADD)
-            square = squares.tile([P, T], F32, name="square", align_bytes=64)
-            nc.scalar.activation(square[:], h, ACT.Square)
-            return square
-
-        def normalize(s):
-            if s < EARLY:
-                square = look_up(s, KB - 1)
-                nc.tensor.matmul(means[s][:], mean_weights[:], square[:], start=False, stop=True)
-                r = root(means[s])
-            else:
-                h_tiles.append(hidden.tile([P, KB, T], F32, name="h"))
-                total = look_up(s, 0)
-                for k in range(1, KB):
-                    square = look_up(s, k)
-                    nc.vector.tensor_tensor(total[:], total[:], square[:], ADD)
-                if s < LATE:
-                    mean = psum.tile([P, T], F32, name="mean", tag="bank")
-                    nc.tensor.matmul(mean[:], mean_weights[:], total[:], start=True, stop=True)
-                    r = root(mean)
-                else:
-                    r = root_by_transposes(total)
-            nc.sync.dma_start(
-                out[0:D, s * T : (s + 1) * T].rearrange("(p k) t -> p k t", k=KB), h_tiles[s][:]
-            )
+        def scale(s, r, cols):
+            width = cols.stop - cols.start
             xs = []
             for k in range(KB):
-                x = norm.tile([P, T], BF16, name=f"x{k}")
+                x = norm.tile([P, width], BF16, name=f"x{k}", tag=f"x{k}_{width}")
                 nc.vector.scalar_tensor_tensor(
-                    x[:], h_tiles[s][:, k, :], gain_cols[k], r[:], MULT, MULT
+                    x[:], h_tiles[s][:, k, cols], gain_cols[k], r[:], MULT, MULT
                 )
                 xs.append(x)
             return xs
 
-        def project(s, xs):
-            y = staged.tile([P, MB, T], F32, name="y")
-            for m in range(MB):
-                acc = psum.tile([P, T], F32, name="acc", tag="bank")
+        def normalize(s):
+            xs_of_pieces = []
+            if s < EARLY:
+                for cols in pieces_of(s):
+                    square = squares.tile([P, T], F32, name="square")
+                    look_up(s, KB - 1, cols, square[:, cols])
+                    mean = means[s, cols.start]
+                    nc.tensor.matmul(mean[:, cols], mean_weights[:], square[:, cols], start=False, stop=True)
+                    xs_of_pieces.append(scale(s, root(mean, cols), cols))
+            else:
+                h_tiles.append(hidden.tile([P, KB, T], F32, name="h"))
+                square_blocks = four.tile([P, KB, T], F32, name="square_blocks", align_bytes=64)
                 for k in range(KB):
-                    nc.tensor.matmul(
-                        acc[:], weight_blocks[m][:, k, :], xs[k][:], start=(k == 0), stop=(k == KB - 1)
-                    )
-                nc.scalar.activation(y[:, m, :], acc[:], ACT.Identity, bias=bias_cols[m])
-                nc.sync.dma_start(out[D + m * P : D + (m + 1) * P, s * T : (s + 1) * T], y[:, m, :])
+                    look_up(s, k, whole, square_blocks[:, k, :])
+                pair = square_blocks[:, 0 : KB // 2, :]
+                nc.vector.tensor_tensor(pair, pair, square_blocks[:, KB // 2 : KB, :], ADD)
+                total = square_blocks[:, 0, :]
+                nc.vector.tensor_tensor(total, total, square_blocks[:, 1, :], ADD)
+                if s < LATE:
+                    mean = psum.tile([P, T], F32, name="mean", tag="bank")
+                    nc.tensor.matmul(mean[:], mean_weights[:], total, start=True, stop=True)
+                    r = root(mean, whole)
+                else:
+                    r = root_by_transposes(total)
+                xs_of_pieces.append(scale(s, r, whole))
+            nc.sync.dma_start(
+                out[0:D, s * T : (s + 1) * T].rearrange("(p k) t -> p k t", k=KB), h_tiles[s][:]
+            )
+            return xs_of_pieces
+
+        def project(s, m, xs, y, cols, done):
+            acc = psum.tile([P, T], F32, name="acc", tag="bank")
+            for k in range(KB):
+                nc.tensor.matmul(
+                    acc[:, cols],
+                    weight_blocks[m][:, k, :],
+                    xs[k][:, cols.start - done : cols.stop - done],
+                    start=(k == 0),
+                    stop=(k == KB - 1),
+                )
+            nc.scalar.activation(y[:, m, cols], acc[:, cols], ACT.Identity, bias=bias_cols[m])
+
+        def store(s, m, y, cols):
+            rows = slice(D + m * P, D + (m + 1) * P)
+            nc.sync.dma_start(out[rows, s * T + cols.start : s * T + cols.stop], y[:, m, cols])
 
         for s in range(EARLY):
             h_tiles.append(hidden.tile([P, KB, T], F32, name="h"))
-            means.append(psum.tile([P, T], F32, name="mean", tag="bank"))
+            for cols in pieces_of(s):
+                means[s, cols.start] = psum.tile([P, T], F32, name="mean", tag="bank")
         for k in range(KB - 1):
             for s in range(EARLY):
-                square = look_up(s, k)
-                nc.tensor.matmul(means[s][:], mean_weights[:], square[:], start=(k == 0), stop=False)
+                square = squares.tile([P, T], F32, name="square")
+                look_up(s, k, whole, square[:])
+                for cols in pieces_of(s):
+                    nc.tensor.matmul(
+                        means[s, cols.start][:, cols], mean_weights[:], square[:, cols], start=(k == 0), stop=False
+                    )
 
-        xs_next = normalize(0)
+        upcoming = normalize(0)
         for s in range(SEQS):
-            xs_now = xs_next
+            xs_of_pieces = upcoming
             if s + 1 < SEQS:
-                xs_next = normalize(s + 1)
-            project(s, xs_now)
+                upcoming = normalize(s + 1)
+            y = staged.tile([P, MB, T], F32, name="y")
+            for cols, xs in zip(pieces_of(s), xs_of_pieces):
+                for m in range(MB):
+                    project(s, m, xs, y, cols, cols.start)
+                    if cols.stop == T:
+                        store(s, m, y, whole)

@@ -14,7 +14,8 @@ SEQS = N // T
 QUAD = 32
 HALF = T // 2
 EARLY = 3
-LATE = 6
+LATE = 5
+TAIL = P
 
 FLOPS = 2 * D * (D + HD + D) * N
 
@@ -23,7 +24,7 @@ def tile_repro_b_kernel(tc, emb, pos, gain, wq, bq, wk, bk, wv, bv, offs, out):
     nc = tc.nc
     with (
         tc.tile_pool(name="held", bufs=1) as held,
-        tc.tile_pool(name="hidden", bufs=EARLY) as hidden,
+        tc.tile_pool(name="hidden", bufs=EARLY + 1) as hidden,
         tc.tile_pool(name="squares", bufs=8) as squares,
         tc.tile_pool(name="norm", bufs=3) as norm,
         tc.tile_pool(name="four", bufs=1) as four,
@@ -195,6 +196,11 @@ def tile_repro_b_kernel(tc, emb, pos, gain, wq, bq, wk, bk, wv, bv, offs, out):
             y = staged.tile([P, MB, T], F32, name="y")
             for cols, xs in zip(pieces_of(s), xs_of_pieces):
                 for m in range(MB):
+                    if (s, m) == (SEQS - 1, MB - 1):
+                        for cut in (slice(0, T - TAIL), slice(T - TAIL, T)):
+                            project(s, m, xs, y, cut, 0)
+                            store(s, m, y, cut)
+                        continue
                     project(s, m, xs, y, cols, cols.start)
                     if cols.stop == T:
                         store(s, m, y, whole)

@@ -14,7 +14,7 @@ SEQS = N // T
 QUAD = 32
 HALF = T // 2
 EARLY = 3
-LATE = 5
+BY_MATMUL = EARLY + 1
 TAIL = P
 
 FLOPS = 2 * D * (D + HD + D) * N
@@ -147,7 +147,7 @@ def tile_repro_b_kernel(tc, emb, pos, gain, wq, bq, wk, bk, wv, bv, offs, out):
                 nc.vector.tensor_tensor(pair, pair, square_blocks[:, KB // 2 : KB, :], ADD)
                 total = square_blocks[:, 0, :]
                 nc.vector.tensor_tensor(total, total, square_blocks[:, 1, :], ADD)
-                if s < LATE:
+                if s == BY_MATMUL:
                     mean = psum.tile([P, T], F32, name="mean", tag="bank")
                     nc.tensor.matmul(mean[:], mean_weights[:], total, start=True, stop=True)
                     r = root(mean, whole)

@@ -12,7 +12,7 @@ KB = D // P
 MB = (D + HD + D) // P
 SEQS = N // T
 QUAD = 32
-HALF = T // 2
+FIRST = 3 * T // 8
 EARLY = 3
 BY_MATMUL = EARLY + 1
 TAIL = P
@@ -40,28 +40,33 @@ def tile_repro_b_kernel(tc, emb, pos, gain, wq, bq, wk, bk, wv, bv, offs, out):
         pos_blocks, tables = [], []
         for k in range(KB):
             pos_block = held.tile([P, T], F32, name=f"pos{k}")
-            ahead = T if k < KB - 1 else HALF
+            ahead = T if k < KB - 1 else FIRST
             nc.sync.dma_start(pos_block[:, 0:ahead], pos_rows[k][:, 0:ahead])
             pos_blocks.append(pos_block)
             table = held.tile([P, V], F32, name=f"table{k}")
             nc.sync.dma_start(table[:], emb_rows[k])
             tables.append(table)
-        nc.sync.dma_start(pos_blocks[KB - 1][:, HALF:T], pos_rows[KB - 1][:, HALF:T])
+        nc.sync.dma_start(pos_blocks[KB - 1][:, FIRST:T], pos_rows[KB - 1][:, FIRST:T])
 
         gains = held.tile([P, KB], F32, name="gains")
         nc.sync.dma_start(gains[:], gain.rearrange("(p k) o -> p (k o)", k=KB))
         gain_cols = [gains[:, k : k + 1] for k in range(KB)]
 
-        weight_blocks = []
+        weight_blocks, out_blocks = [], []
+        first = D
         for label, w in (("wq", wq), ("wk", wk), ("wv", wv)):
             w_sb = held.tile([P, KB, w.shape[1]], BF16, name=label + "_sb")
             nc.sync.dma_start(w_sb[:], w.rearrange("(p k) m -> p k m", k=KB))
-            weight_blocks.extend([w_sb[:, :, a * P : (a + 1) * P] for a in range(w.shape[1] // P)])
+            blocks = w.shape[1] // P
+            rows = out[first : first + w.shape[1], :].rearrange("(q a) j -> a q j", a=blocks)
+            weight_blocks.extend([w_sb[:, :, a::blocks] for a in range(blocks)])
+            out_blocks.extend([rows[a] for a in range(blocks)])
+            first += w.shape[1]
 
         bias_cols = []
         for label, vec in (("bq", bq), ("bk", bk), ("bv", bv)):
             cols = held.tile([P, vec.shape[0] // P], F32, name=label + "_cols")
-            nc.sync.dma_start(cols[:], vec.rearrange("(a p) o -> p (a o)", p=P))
+            nc.sync.dma_start(cols[:], vec.rearrange("(q a) o -> q (a o)", q=P))
             bias_cols.extend([cols[:, a : a + 1] for a in range(cols.shape[1])])
 
         mean_weights = held.tile([P, P], F32, name="mean_weights")
@@ -84,7 +89,7 @@ def tile_repro_b_kernel(tc, emb, pos, gain, wq, bq, wk, bk, wv, bv, offs, out):
         whole = slice(0, T)
 
         def pieces_of(s):
-            return [slice(0, HALF), slice(HALF, T)] if s == 0 else [whole]
+            return [slice(0, FIRST), slice(FIRST, T)] if s == 0 else [whole]
 
         h_tiles, means = [], {}
 
@@ -172,8 +177,7 @@ def tile_repro_b_kernel(tc, emb, pos, gain, wq, bq, wk, bk, wv, bv, offs, out):
             nc.scalar.activation(y[:, m, cols], acc[:, cols], ACT.Identity, bias=bias_cols[m])
 
         def store(s, m, y, cols):
-            rows = slice(D + m * P, D + (m + 1) * P)
-            nc.sync.dma_start(out[rows, s * T + cols.start : s * T + cols.stop], y[:, m, cols])
+            nc.sync.dma_start(out_blocks[m][:, s * T + cols.start : s * T + cols.stop], y[:, m, cols])
 
         for s in range(EARLY):
             h_tiles.append(hidden.tile([P, KB, T], F32, name="h"))

import concourse.mybir as mybir

F32, BF16, U16 = mybir.dt.float32, mybir.dt.bfloat16, mybir.dt.uint16
ADD, MULT, NOT_EQUAL = mybir.AluOpType.add, mybir.AluOpType.mult, mybir.AluOpType.not_equal
X_AXIS = mybir.AxisListType.X
ACT = mybir.ActivationFunctionType

P = 128
D, V, T, HD, N = 512, 4096, 512, 128, 4096
EPS = 1.1920928955078125e-07
KB = D // P
MB = (D + HD + D) // P
SEQS = N // T
QUAD = 32
FIRST = 3 * T // 8
EARLY = 3
BY_MATMUL = EARLY + 1
TAIL = P

FLOPS = 2 * D * (D + HD + D) * N


def tile_repro_b_kernel(tc, emb, pos, gain, wq, bq, wk, bk, wv, bv, offs, out):
    nc = tc.nc
    with (
        tc.tile_pool(name="held", bufs=1) as held,
        tc.tile_pool(name="hidden", bufs=EARLY + 1) as hidden,
        tc.tile_pool(name="squares", bufs=8) as squares,
        tc.tile_pool(name="norm", bufs=3) as norm,
        tc.tile_pool(name="four", bufs=1) as four,
        tc.tile_pool(name="turn", bufs=2) as turn,
        tc.tile_pool(name="staged", bufs=2) as staged,
        tc.psum_pool(name="psum", bufs=8) as psum,
    ):
        offsets = held.tile([P, N // 16], U16, name="offsets")
        nc.sync.dma_start(offsets[:], offs)

        pos_rows = pos.rearrange("(p k) t -> k p t", k=KB)
        emb_rows = emb.rearrange("(p k) v -> k p v", k=KB)
        pos_blocks, tables = [], []
        for k in range(KB):
            pos_block = held.tile([P, T], F32, name=f"pos{k}")
            ahead = T if k < KB - 1 else FIRST
            nc.sync.dma_start(pos_block[:, 0:ahead], pos_rows[k][:, 0:ahead])
            pos_blocks.append(pos_block)
            table = held.tile([P, V], F32, name=f"table{k}")
            nc.sync.dma_start(table[:], emb_rows[k])
            tables.append(table)
        nc.sync.dma_start(pos_blocks[KB - 1][:, FIRST:T], pos_rows[KB - 1][:, FIRST:T])

        gains = held.tile([P, KB], F32, name="gains")
        nc.sync.dma_start(gains[:], gain.rearrange("(p k) o -> p (k o)", k=KB))
        gain_cols = [gains[:, k : k + 1] for k in range(KB)]

        weight_blocks, out_blocks = [], []
        first = D
        for label, w in (("wq", wq), ("wk", wk), ("wv", wv)):
            w_sb = held.tile([P, KB, w.shape[1]], BF16, name=label + "_sb")
            nc.sync.dma_start(w_sb[:], w.rearrange("(p k) m -> p k m", k=KB))
            blocks = w.shape[1] // P
            rows = out[first : first + w.shape[1], :].rearrange("(q a) j -> a q j", a=blocks)
            weight_blocks.extend([w_sb[:, :, a::blocks] for a in range(blocks)])
            out_blocks.extend([rows[a] for a in range(blocks)])
            first += w.shape[1]

        bias_cols = []
        for label, vec in (("bq", bq), ("bk", bk), ("bv", bv)):
            cols = held.tile([P, vec.shape[0] // P], F32, name=label + "_cols")
            nc.sync.dma_start(cols[:], vec.rearrange("(q a) o -> q (a o)", q=P))
            bias_cols.extend([cols[:, a : a + 1] for a in range(cols.shape[1])])

        mean_weights = held.tile([P, P], F32, name="mean_weights")
        nc.vector.memset(mean_weights[:], 1.0 / D)
        quad_weights = held.tile([P, P], F32, name="quad_weights")
        nc.gpsimd.memset(quad_weights[:], 0.0)
        for shift in range(QUAD - P, P, QUAD):
            nc.gpsimd.affine_select(
                out=quad_weights[:],
                in_=quad_weights[:],
                pattern=[[-1, P]],
                compare_op=NOT_EQUAL,
                fill=1.0 / D,
                base=shift,
                channel_multiplier=1,
            )
        eps_col = held.tile([P, 1], F32, name="eps_col")
        nc.vector.memset(eps_col[:], EPS)

        whole = slice(0, T)

        def pieces_of(s):
            return [slice(0, FIRST), slice(FIRST, T)] if s == 0 else [whole]

        h_tiles, means = [], {}

        def look_up(s, k, cols, square):
            h = h_tiles[s][:, k, cols]
            piece = offsets[:, (s * T + cols.start) // 16 : (s * T + cols.stop) // 16]
            nc.vector.tensor_tensor(h, tables[k][:].indirect(piece), pos_blocks[k][:, cols], ADD)
            nc.scalar.activation(square, h, ACT.Square)

        def root(mean, cols):
            width = cols.stop - cols.start
            r = norm.tile([P, width], F32, name="r", tag=f"r{width}", align_bytes=64)
            nc.scalar.activation(r[:], mean[:, cols], ACT.Abs_reciprocal_sqrt, bias=eps_col[:])
            return r

        def root_by_transposes(total):
            turned = turn.tile([P, T], F32, name="turned", align_bytes=64)
            nc.vector.transpose(turned[:], total)
            part = turn.tile([P, T // QUAD], F32, name="part")
            nc.vector.tensor_reduce(part[:], turned[:].rearrange("p (b i) -> p b i", i=QUAD), X_AXIS, ADD)
            narrow = psum.tile([P, T // QUAD], F32, name="narrow", tag="bank")
            nc.tensor.matmul(narrow[:], quad_weights[:], part[:], start=True, stop=True)
            spread = turn.tile([P, T // QUAD, QUAD], F32, name="spread", align_bytes=64)
            nc.scalar.activation(
                spread[:],
                narrow[:].unsqueeze(2).to_broadcast([P, T // QUAD, QUAD]),
                ACT.Abs_reciprocal_sqrt,
                bias=eps_col[:],
            )
            r = norm.tile([P, T], F32, name="r", tag=f"r{T}", align_bytes=64)
            nc.vector.transpose(r[:], spread[:].rearrange("p b i -> p (b i)"))
            return r

        def scale(s, r, cols):
            width = cols.stop - cols.start
            xs = []
            for k in range(KB):
                x = norm.tile([P, width], BF16, name=f"x{k}", tag=f"x{k}_{width}")
                nc.vector.scalar_tensor_tensor(
                    x[:], h_tiles[s][:, k, cols], gain_cols[k], r[:], MULT, MULT
                )
                xs.append(x)
            return xs

        def normalize(s):
            xs_of_pieces = []
            if s < EARLY:
                for cols in pieces_of(s):
                    square = squares.tile([P, T], F32, name="square")
                    look_up(s, KB - 1, cols, square[:, cols])
                    mean = means[s, cols.start]
                    nc.tensor.matmul(mean[:, cols], mean_weights[:], square[:, cols], start=False, stop=True)
                    xs_of_pieces.append(scale(s, root(mean, cols), cols))
            else:
                h_tiles.append(hidden.tile([P, KB, T], F32, name="h"))
                square_blocks = four.tile([P, KB, T], F32, name="square_blocks", align_bytes=64)
                for k in range(KB):
                    look_up(s, k, whole, square_blocks[:, k, :])
                pair = square_blocks[:, 0 : KB // 2, :]
                nc.vector.tensor_tensor(pair, pair, square_blocks[:, KB // 2 : KB, :], ADD)
                total = square_blocks[:, 0, :]
                nc.vector.tensor_tensor(total, total, square_blocks[:, 1, :], ADD)
                if s == BY_MATMUL:
                    mean = psum.tile([P, T], F32, name="mean", tag="bank")
                    nc.tensor.matmul(mean[:], mean_weights[:], total, start=True, stop=True)
                    r = root(mean, whole)
                else:
                    r = root_by_transposes(total)
                xs_of_pieces.append(scale(s, r, whole))
            nc.sync.dma_start(
                out[0:D, s * T : (s + 1) * T].rearrange("(p k) t -> p k t", k=KB), h_tiles[s][:]
            )
            return xs_of_pieces

        def project(s, m, xs, y, cols, done):
            acc = psum.tile([P, T], F32, name="acc", tag="bank")
            for k in range(KB):
                nc.tensor.matmul(
                    acc[:, cols],
                    weight_blocks[m][:, k, :],
                    xs[k][:, cols.start - done : cols.stop - done],
                    start=(k == 0),
                    stop=(k == KB - 1),
                )
            nc.scalar.activation(y[:, m, cols], acc[:, cols], ACT.Identity, bias=bias_cols[m])

        def store(s, m, y, cols):
            nc.sync.dma_start(out_blocks[m][:, s * T + cols.start : s * T + cols.stop], y[:, m, cols])

        for s in range(EARLY):
            h_tiles.append(hidden.tile([P, KB, T], F32, name="h"))
            for cols in pieces_of(s):
                means[s, cols.start] = psum.tile([P, T], F32, name="mean", tag="bank")
        for k in range(KB - 1):
            for s in range(EARLY):
                square = squares.tile([P, T], F32, name="square")
                look_up(s, k, whole, square[:])
                for cols in pieces_of(s):
                    nc.tensor.matmul(
                        means[s, cols.start][:, cols], mean_weights[:], square[:, cols], start=(k == 0), stop=False
                    )

        upcoming = normalize(0)
        for s in range(SEQS):
            xs_of_pieces = upcoming
            if s + 1 < SEQS:
                upcoming = normalize(s + 1)
            y = staged.tile([P, MB, T], F32, name="y")
            for cols, xs in zip(pieces_of(s), xs_of_pieces):
                for m in range(MB):
                    if (s, m) == (SEQS - 1, MB - 1):
                        for cut in (slice(0, T - TAIL), slice(T - TAIL, T)):
                            project(s, m, xs, y, cut, 0)
                            store(s, m, y, cut)
                        continue
                    project(s, m, xs, y, cols, cols.start)
                    if cols.stop == T:
                        store(s, m, y, whole)
